import numpy as np
import ml_dtypes


def mxq(x, axis, fmt="e4m3"):
    dtype, down = {"e4m3": (ml_dtypes.float8_e4m3fn, 7), "e5m2": (ml_dtypes.float8_e5m2, 14)}[fmt]
    v = np.moveaxis(np.asarray(x, np.float32).astype(ml_dtypes.bfloat16).astype(np.float64), axis, -1)
    blocks = v.reshape(v.shape[:-1] + (-1, 32))
    amax = np.abs(blocks).max(-1, keepdims=True)
    byte = np.maximum(np.where(amax > 0, np.frexp(amax)[1] - 1 + 127, 0) - down, 1)
    scale = np.exp2(byte - 127.0)
    codes = (blocks / scale).astype(np.float32).astype(dtype).astype(np.float64)
    return np.moveaxis((codes * scale).reshape(v.shape), -1, axis)


WIDE = False


def mx_kscale(k):
    if not WIDE:
        return np.ones(k)
    levels = np.array([10, -10, 5, -5, 0])
    a = np.random.permutation(np.resize(levels, k // 512 * 4)).reshape(k // 512, 4)
    idx = np.arange(k)
    return np.exp2(a[idx // 512, idx % 128 // 32])


BF16 = ml_dtypes.bfloat16


def bf(x):
    return np.asarray(x, np.float32).astype(BF16)


def f64(x):
    return np.asarray(x).astype(np.float64)


B, T, N, C, ORDER, KT = 1, 6, 1024, 128, 4, 3
CO = C * ORDER
J = 2 * C


def sigmoid(v):
    return 1.0 / (1.0 + np.exp(-v))


def setup_inputs():
    f = mx_kscale(CO)[::ORDER]
    fr = np.tile(np.repeat(f, ORDER), KT)
    g = np.concatenate([f, np.ones(C)])
    return {"inputs": bf(np.random.standard_normal((B, T, N, C)) * f),
            "supports": bf(np.random.standard_normal((N, ORDER * N)) / np.sqrt(N)),
            "weights": bf(np.random.standard_normal((KT * CO, J)) / np.sqrt(KT * CO) / fr[:, None] * g),
            "biases": bf(np.random.standard_normal(J) * 0.3 * g)}


def reference(inputs, supports, weights, biases):
    x = f64(inputs)
    a = mxq(x, 2, "e4m3").transpose(0, 1, 3, 2) @ mxq(f64(supports), 0, "e4m3")
    z = a.reshape(B, T, C, ORDER, N).transpose(0, 1, 4, 2, 3).reshape(B, T, N, CO)
    zq = mxq(z, 3, "e4m3")
    wq = mxq(f64(weights).reshape(KT, CO, J), 1, "e4m3")
    conv = np.zeros((B, T, N, J)) + f64(biases)
    for k in range(KT):
        lag = KT - 1 - k
        conv[:, lag:] += (zq[:, :T - lag] @ wq[k])
    return (conv[..., :C] + x) * sigmoid(conv[..., C:])

@@ -1,0 +1,249 @@
+from contextlib import ExitStack
+
+import concourse.mybir as mybir
+
+BF16 = mybir.dt.bfloat16
+F32 = mybir.dt.float32
+U32 = mybir.dt.uint32
+U8 = mybir.dt.uint8
+FP8X4 = mybir.dt.float8_e4m3fn_x4
+ACT = mybir.ActivationFunctionType
+ALU = mybir.AluOpType
+
+P = 128
+T = 6
+NODES = 1024
+C = 128
+ORDER = 4
+KT = 3
+J = 2 * C
+NB = NODES // P
+KP = 2
+FLOPS = 2 * T * C * NODES * ORDER * NODES + 2 * T * NODES * KT * C * ORDER * J
+
+MANUAL = False
+CHUNKS = [(0, 128), (128, 128), (256, 256), (512, 256), (768, 256)]
+EPI = [(0, 4), (4, 6)]
+
+
+def tile_conv_st_pa_kernel(tc, inputs, supports, weights, biases, out):
+    nc = tc.nc
+    with ExitStack() as ctx:
+        if MANUAL:
+            ctx.enter_context(tc.manual_schedule())
+        keep = ctx.enter_context(tc.tile_pool(name="keep", bufs=1))
+        grp_pool = ctx.enter_context(tc.tile_pool(name="grp", bufs=2))
+        sq_pool = ctx.enter_context(tc.tile_pool(name="sq", bufs=3))
+        z_pool = ctx.enter_context(tc.tile_pool(name="z", bufs=2))
+        zq_pool = ctx.enter_context(tc.tile_pool(name="zq", bufs=3))
+        y_pool = ctx.enter_context(tc.tile_pool(name="y", bufs=2))
+        ps1 = ctx.enter_context(tc.psum_pool(name="ps1", bufs=5))
+        ps2 = ctx.enter_context(tc.psum_pool(name="ps2", bufs=3))
+
+        ones = keep.tile([P, P], BF16, name="ones")
+        nc.vector.memset(ones[:], 1.0)
+        brow = keep.tile([P, J], BF16, name="brow")
+        nc.vector.memset(brow[:], 0.0)
+
+        x_raw = keep.tile([P, T, NB, C], BF16, name="x_raw")
+        xv = inputs.rearrange("a t (b p) c -> p (a t) b c", p=P)
+        sv = supports.rearrange("(b p) (o n) -> p b o n", p=P, o=ORDER)
+        s_raw = []
+        for ci, (n0, nw) in enumerate(CHUNKS):
+            s_raw.append(keep.tile([P, NB, ORDER, nw], BF16, name="s_raw%d" % ci))
+        w_raw = keep.tile([P, KT, ORDER, J], BF16, name="w_raw")
+
+        def load_x(h):
+            nc.sync.dma_start(out=x_raw[:, 2 * h:2 * h + 2], in_=xv[:, 2 * h:2 * h + 2])
+
+        def load_s(ci):
+            n0, nw = CHUNKS[ci]
+            for o in range(ORDER):
+                nc.sync.dma_start(out=s_raw[ci][:, :, o, :], in_=sv[:, :, o, n0:n0 + nw])
+
+        load_x(0)
+        load_s(0)
+        load_x(1)
+        load_x(2)
+        nc.sync.dma_start(out=brow[0:1, :], in_=biases.rearrange("(a n) -> a n", a=1))
+        nc.sync.dma_start(
+            out=w_raw[:].rearrange("p k j n -> p k (j n)"),
+            in_=weights.rearrange("(k p j) n -> p k (j n)", k=KT, p=P, j=ORDER),
+        )
+        for ci in range(1, len(CHUNKS)):
+            load_s(ci)
+
+        xg = keep.tile([P, T, KP, C, 4], BF16, name="xg", align_bytes=64)
+        xq = keep.tile([P, T, KP, C], U32, name="xq", align_bytes=64)
+        xs = keep.tile([P, T, KP, C], U8, name="xs", align_bytes=64)
+
+        def prep_x(h, eng_copy):
+            sl = slice(2 * h, 2 * h + 2)
+            eng_copy(
+                out=xg[:, sl].rearrange("p t k (c i) j -> p (t k) c j i", i=4),
+                in_=x_raw[:, sl].rearrange("p t (k j) (c i) -> p (t k) c j i", j=4, i=4),
+            )
+
+        def quant_x(h):
+            sl = slice(2 * h, 2 * h + 2)
+            nc.vector.quantize_mx(
+                out=xq[:, sl].rearrange("p t k c -> p (t k c)").bitcast(FP8X4),
+                scales=xs[:, sl].rearrange("p t k c -> p (t k c)"),
+                in_=xg[:, sl].rearrange("p t k c j -> p (t k c j)"),
+            )
+
+        wg = keep.tile([P, KT, J, 4], BF16, name="wg", align_bytes=64)
+        wq = keep.tile([P, KT, J], U32, name="wq", align_bytes=64)
+        ws = keep.tile([P, KT, J], U8, name="ws", align_bytes=64)
+        bb = keep.tile([P, J], F32, name="bb")
+
+        blk_src = []
+        for ci, (n0, nw) in enumerate(CHUNKS):
+            for q in range(nw // P):
+                blk_src.append((ci, q))
+        grp_t = {}
+        sq_t = {}
+
+        def regroup_s(b, kp, eng_copy):
+            ci, q = blk_src[b]
+            if kp == 0:
+                grp_t[b] = grp_pool.tile([P, KP, ORDER, P, 4], BF16, name="grp", align_bytes=64)
+            eng_copy(
+                out=grp_t[b][:, kp].rearrange("p o (c i) j -> p o c j i", i=4),
+                in_=s_raw[ci][:, 4 * kp:4 * kp + 4, :, q * P:(q + 1) * P].rearrange(
+                    "p j o (c i) -> p o c j i", i=4),
+            )
+
+        def quant_s(b, kp):
+            if kp == 0:
+                sqc = sq_pool.tile([P, KP, ORDER * P], U32, name="sqc", align_bytes=64)
+                sqs = sq_pool.tile([P, KP, ORDER * P], U8, name="sqs", align_bytes=64)
+                sq_t[b] = (sqc, sqs)
+            sqc, sqs = sq_t[b]
+            nc.vector.quantize_mx(
+                out=sqc[:, kp].bitcast(FP8X4),
+                scales=sqs[:, kp],
+                in_=grp_t[b][:, kp].rearrange("p o n j -> p (o n j)"),
+            )
+
+        z_t = {}
+        zq_t = {}
+        y_t = {}
+        cb_t = {}
+
+        def step1(b, t):
+            if t == 0:
+                z_t[b] = z_pool.tile([P, T, P, ORDER], BF16, name="zb", align_bytes=64)
+                zqc = zq_pool.tile([P, T, P], U32, name="zqc", align_bytes=64)
+                zqs = zq_pool.tile([P, T, P], U8, name="zqs", align_bytes=64)
+                zq_t[b] = (zqc, zqs)
+            sqc, sqs = sq_t[b]
+            bank = ps1.tile([P, ORDER * P], F32, name="zbank")
+            for kp in range(KP):
+                nc.tensor.matmul_mx(
+                    out=bank[:],
+                    lhsT=xq[:, t, kp].bitcast(FP8X4),
+                    lhsT_scale=xs[:, t, kp],
+                    rhs=sqc[:, kp].bitcast(FP8X4),
+                    rhs_scale=sqs[:, kp],
+                    start=(kp == 0),
+                    stop=(kp == KP - 1),
+                )
+            nc.scalar.copy(out=z_t[b][:, t], in_=bank[:].rearrange("p (o n) -> p n o", o=ORDER))
+            if t % 2 == 1:
+                sl = slice(t - 1, t + 1)
+                zqc, zqs = zq_t[b]
+                nc.vector.quantize_mx(
+                    out=zqc[:, sl].rearrange("p t n -> p (t n)").bitcast(FP8X4),
+                    scales=zqs[:, sl].rearrange("p t n -> p (t n)"),
+                    in_=z_t[b][:, sl].rearrange("p t n o -> p (t n o)"),
+                )
+
+        def step2(b, t):
+            if t == 0:
+                y_t[b] = y_pool.tile([P, T, J], F32, name="y")
+            if t % 2 == 0:
+                cb_t[b] = ps2.tile([P, 2, J], F32, name="cb")
+            zqc, zqs = zq_t[b]
+            taps = [k for k in range(KT) if t - (KT - 1) + k >= 0]
+            for k in taps:
+                tz = t - (KT - 1) + k
+                nc.tensor.matmul_mx(
+                    out=cb_t[b][:, t % 2],
+                    lhsT=zqc[:, tz].bitcast(FP8X4),
+                    lhsT_scale=zqs[:, tz],
+                    rhs=wq[:, k].bitcast(FP8X4),
+                    rhs_scale=ws[:, k],
+                    start=(k == taps[0]),
+                    stop=(k == taps[-1]),
+                )
+            if t % 2 == 1:
+                nc.vector.tensor_tensor(
+                    out=y_t[b][:, t - 1:t + 1],
+                    in0=cb_t[b][:],
+                    in1=bb[:].unsqueeze(1).to_broadcast([P, 2, J]),
+                    op=ALU.add,
+                )
+
+        ov = out.rearrange("a t (b p) c -> p b (a t) c", p=P)
+        ot_t = {}
+
+        def epilogue(b, g):
+            t0, t1 = EPI[g]
+            y = y_t[b]
+            if g == 0:
+                ot_t[b] = y_pool.tile([P, T, C], F32, name="ot")
+            nc.scalar.activation(out=y[:, t0:t1, C:J], in_=y[:, t0:t1, C:J], func=ACT.Sigmoid)
+            nc.vector.tensor_tensor(
+                out=y[:, t0:t1, 0:C], in0=y[:, t0:t1, 0:C], in1=x_raw[:, t0:t1, b, :], op=ALU.add)
+            nc.vector.tensor_tensor(
+                out=ot_t[b][:, t0:t1], in0=y[:, t0:t1, 0:C], in1=y[:, t0:t1, C:J], op=ALU.mult)
+            if g == len(EPI) - 1:
+                nc.sync.dma_start(out=ov[:, b], in_=ot_t[b][:])
+
+        prep_x(0, nc.vector.tensor_copy)
+        regroup_s(0, 0, nc.vector.tensor_copy)
+        regroup_s(0, 1, nc.scalar.copy)
+        quant_x(0)
+        quant_s(0, 0)
+        prep_x(1, nc.scalar.copy)
+        prep_x(2, nc.vector.tensor_copy)
+        quant_s(0, 1)
+        quant_x(1)
+        quant_x(2)
+        bps = ps2.tile([P, 2, J], F32, name="cb")
+        nc.tensor.matmul(out=bps[:, 0], lhsT=ones[:], rhs=brow[:], start=True, stop=True)
+        nc.vector.tensor_copy(out=bb[:], in_=bps[:, 0])
+        nc.scalar.copy(
+            out=wg[:].rearrange("p k (c i) j -> p k c j i", i=4),
+            in_=w_raw[:].rearrange("p k j (c i) -> p k c j i", i=4),
+        )
+        nc.vector.quantize_mx(
+            out=wq[:, 0:2].rearrange("p k n -> p (k n)").bitcast(FP8X4),
+            scales=ws[:, 0:2].rearrange("p k n -> p (k n)"),
+            in_=wg[:, 0:2].rearrange("p k n j -> p (k n j)"),
+        )
+        nc.vector.quantize_mx(
+            out=wq[:, 2].bitcast(FP8X4),
+            scales=ws[:, 2],
+            in_=wg[:, 2].rearrange("p n j -> p (n j)"),
+        )
+
+        for s in range(NB + 1):
+            for t in range(T):
+                if s + 1 < NB:
+                    if t == 0:
+                        regroup_s(s + 1, 0, nc.vector.tensor_copy)
+                    if t == 1:
+                        regroup_s(s + 1, 1, nc.scalar.copy)
+                    if t == 2:
+                        quant_s(s + 1, 0)
+                    if t == 4:
+                        quant_s(s + 1, 1)
+                if s < NB:
+                    step1(s, t)
+                if s >= 1:
+                    step2(s - 1, t)
+                    for g, (t0, t1) in enumerate(EPI):
+                        if t == t1 - 1:
+                            epilogue(s - 1, g)

@@ -19,11 +19,18 @@ KT = 3
 J = 2 * C
 NB = NODES // P
 KP = 2
+NPAIR = T // 2
 FLOPS = 2 * T * C * NODES * ORDER * NODES + 2 * T * NODES * KT * C * ORDER * J
 
 MANUAL = False
-CHUNKS = [(0, 128), (128, 128), (256, 256), (512, 256), (768, 256)]
-EPI = [(0, 4), (4, 6)]
+L2 = 4
+CW = 256
+NCH = NODES // CW
+BPC = CW // P
+PREP_BASE = [0,0,6,10,16,22,29,35]
+NS = [0,0,2,3,3,3,3,3]
+V3_GP = False
+XB_GP = False
 
 
 def tile_conv_st_pa_kernel(tc, inputs, supports, weights, biases, out):
@@ -32,11 +39,12 @@ def tile_conv_st_pa_kernel(tc, inputs, supports, weights, biases, out):
         if MANUAL:
             ctx.enter_context(tc.manual_schedule())
         keep = ctx.enter_context(tc.tile_pool(name="keep", bufs=1))
-        grp_pool = ctx.enter_context(tc.tile_pool(name="grp", bufs=2))
+        grp_pool = ctx.enter_context(tc.tile_pool(name="grp", bufs=3))
         sq_pool = ctx.enter_context(tc.tile_pool(name="sq", bufs=3))
         z_pool = ctx.enter_context(tc.tile_pool(name="z", bufs=2))
         zq_pool = ctx.enter_context(tc.tile_pool(name="zq", bufs=3))
-        y_pool = ctx.enter_context(tc.tile_pool(name="y", bufs=2))
+        y_pool = ctx.enter_context(tc.tile_pool(name="y", bufs=4))
+        ot_pool = ctx.enter_context(tc.tile_pool(name="ot", bufs=3))
         ps1 = ctx.enter_context(tc.psum_pool(name="ps1", bufs=5))
         ps2 = ctx.enter_context(tc.psum_pool(name="ps2", bufs=3))
 
@@ -49,35 +57,47 @@ def tile_conv_st_pa_kernel(tc, inputs, supports, weights, biases, out):
         xv = inputs.rearrange("a t (b p) c -> p (a t) b c", p=P)
         sv = supports.rearrange("(b p) (o n) -> p b o n", p=P, o=ORDER)
         s_raw = []
-        for ci, (n0, nw) in enumerate(CHUNKS):
-            s_raw.append(keep.tile([P, NB, ORDER, nw], BF16, name="s_raw%d" % ci))
+        for ci in range(NCH):
+            s_raw.append(keep.tile([P, NB, ORDER, CW], BF16, name="s_raw%d" % ci))
         w_raw = keep.tile([P, KT, ORDER, J], BF16, name="w_raw")
 
         def load_x(h):
             nc.sync.dma_start(out=x_raw[:, 2 * h:2 * h + 2], in_=xv[:, 2 * h:2 * h + 2])
 
-        def load_s(ci):
-            n0, nw = CHUNKS[ci]
+        def load_s(ci, kp):
             for o in range(ORDER):
-                nc.sync.dma_start(out=s_raw[ci][:, :, o, :], in_=sv[:, :, o, n0:n0 + nw])
+                nc.sync.dma_start(
+                    out=s_raw[ci][:, 4 * kp:4 * kp + 4, o, :],
+                    in_=sv[:, 4 * kp:4 * kp + 4, o, ci * CW:(ci + 1) * CW],
+                )
 
+        def load_w():
+            nc.sync.dma_start(
+                out=w_raw[:].rearrange("p k j n -> p k (j n)"),
+                in_=weights.rearrange("(k p j) n -> p k (j n)", k=KT, p=P, j=ORDER),
+            )
+
+        nc.sync.dma_start(out=brow[0:1, :], in_=biases.rearrange("(a n) -> a n", a=1))
         load_x(0)
-        load_s(0)
         load_x(1)
         load_x(2)
-        nc.sync.dma_start(out=brow[0:1, :], in_=biases.rearrange("(a n) -> a n", a=1))
-        nc.sync.dma_start(
-            out=w_raw[:].rearrange("p k j n -> p k (j n)"),
-            in_=weights.rearrange("(k p j) n -> p k (j n)", k=KT, p=P, j=ORDER),
-        )
-        for ci in range(1, len(CHUNKS)):
-            load_s(ci)
+        load_s(0, 0)
+        load_s(0, 1)
+        load_w()
+        for ci in range(1, NCH):
+            load_s(ci, 0)
+            load_s(ci, 1)
 
         xg = keep.tile([P, T, KP, C, 4], BF16, name="xg", align_bytes=64)
         xq = keep.tile([P, T, KP, C], U32, name="xq", align_bytes=64)
         xs = keep.tile([P, T, KP, C], U8, name="xs", align_bytes=64)
+        xb = keep.tile([P, NB * NPAIR + 1, 2 * C], F32, name="xb")
+        bv = keep.tile([P, C], F32, name="bv")
+        wg = keep.tile([P, KT, J, 4], BF16, name="wg", align_bytes=64)
+        wq = keep.tile([P, KT, J], U32, name="wq", align_bytes=64)
+        ws = keep.tile([P, KT, J], U8, name="ws", align_bytes=64)
 
-        def prep_x(h, eng_copy):
+        def regroup_x(h, eng_copy):
             sl = slice(2 * h, 2 * h + 2)
             eng_copy(
                 out=xg[:, sl].rearrange("p t k (c i) j -> p (t k) c j i", i=4),
@@ -92,30 +112,52 @@ def tile_conv_st_pa_kernel(tc, inputs, supports, weights, biases, out):
                 in_=xg[:, sl].rearrange("p t k c j -> p (t k c j)"),
             )
 
-        wg = keep.tile([P, KT, J, 4], BF16, name="wg", align_bytes=64)
-        wq = keep.tile([P, KT, J], U32, name="wq", align_bytes=64)
-        ws = keep.tile([P, KT, J], U8, name="ws", align_bytes=64)
-        bb = keep.tile([P, J], F32, name="bb")
+        def make_xb(h):
+            eng = nc.gpsimd if XB_GP else nc.vector
+            eng.tensor_tensor(
+                out=xb[:, h:NB * NPAIR:NPAIR, :].rearrange("p b (t c) -> p b t c", t=2),
+                in0=x_raw[:, 2 * h:2 * h + 2].rearrange("p t b c -> p b t c"),
+                in1=bv[:].unsqueeze(1).unsqueeze(1).to_broadcast([P, NB, 2, C]),
+                op=ALU.add,
+            )
 
-        blk_src = []
-        for ci, (n0, nw) in enumerate(CHUNKS):
-            for q in range(nw // P):
-                blk_src.append((ci, q))
+        def prep_bias():
+            bps = ps2.tile([P, 2, J], F32, name="cb")
+            nc.tensor.matmul(out=bps[:, 0], lhsT=ones[:], rhs=brow[:], start=True, stop=True)
+            nc.vector.tensor_copy(out=bv[:], in_=bps[:, 0, 0:C])
+            nc.vector.tensor_copy(
+                out=xb[:, NB * NPAIR, :].rearrange("p (t c) -> p t c", t=2),
+                in_=bps[:, 0, C:J].unsqueeze(1).to_broadcast([P, 2, C]),
+            )
+
+        def regroup_w(k, eng_copy):
+            eng_copy(
+                out=wg[:, k].rearrange("p (c i) j -> p c j i", i=4),
+                in_=w_raw[:, k].rearrange("p j (c i) -> p c j i", i=4),
+            )
+
+        def quant_w(k):
+            nc.vector.quantize_mx(
+                out=wq[:, k].bitcast(FP8X4),
+                scales=ws[:, k],
+                in_=wg[:, k].rearrange("p n j -> p (n j)"),
+            )
+
         grp_t = {}
         sq_t = {}
 
-        def regroup_s(b, kp, eng_copy):
-            ci, q = blk_src[b]
-            if kp == 0:
+        def regroup_s(b, kp, o0, o1, eng_copy):
+            if b not in grp_t:
                 grp_t[b] = grp_pool.tile([P, KP, ORDER, P, 4], BF16, name="grp", align_bytes=64)
+            ci, q = divmod(b, BPC)
             eng_copy(
-                out=grp_t[b][:, kp].rearrange("p o (c i) j -> p o c j i", i=4),
-                in_=s_raw[ci][:, 4 * kp:4 * kp + 4, :, q * P:(q + 1) * P].rearrange(
+                out=grp_t[b][:, kp, o0:o1].rearrange("p o (c i) j -> p o c j i", i=4),
+                in_=s_raw[ci][:, 4 * kp:4 * kp + 4, o0:o1, q * P:(q + 1) * P].rearrange(
                     "p j o (c i) -> p o c j i", i=4),
             )
 
         def quant_s(b, kp):
-            if kp == 0:
+            if b not in sq_t:
                 sqc = sq_pool.tile([P, KP, ORDER * P], U32, name="sqc", align_bytes=64)
                 sqs = sq_pool.tile([P, KP, ORDER * P], U8, name="sqs", align_bytes=64)
                 sq_t[b] = (sqc, sqs)
@@ -130,6 +172,7 @@ def tile_conv_st_pa_kernel(tc, inputs, supports, weights, biases, out):
         zq_t = {}
         y_t = {}
         cb_t = {}
+        ot_t = {}
 
         def step1(b, t):
             if t == 0:
@@ -150,26 +193,25 @@ def tile_conv_st_pa_kernel(tc, inputs, supports, weights, biases, out):
                     stop=(kp == KP - 1),
                 )
             nc.scalar.copy(out=z_t[b][:, t], in_=bank[:].rearrange("p (o n) -> p n o", o=ORDER))
-            if t % 2 == 1:
-                sl = slice(t - 1, t + 1)
-                zqc, zqs = zq_t[b]
-                nc.vector.quantize_mx(
-                    out=zqc[:, sl].rearrange("p t n -> p (t n)").bitcast(FP8X4),
-                    scales=zqs[:, sl].rearrange("p t n -> p (t n)"),
-                    in_=z_t[b][:, sl].rearrange("p t n o -> p (t n o)"),
-                )
+
+        def quant_z(b, h):
+            sl = slice(2 * h, 2 * h + 2)
+            zqc, zqs = zq_t[b]
+            nc.vector.quantize_mx(
+                out=zqc[:, sl].rearrange("p t n -> p (t n)").bitcast(FP8X4),
+                scales=zqs[:, sl].rearrange("p t n -> p (t n)"),
+                in_=z_t[b][:, sl].rearrange("p t n o -> p (t n o)"),
+            )
 
         def step2(b, t):
-            if t == 0:
-                y_t[b] = y_pool.tile([P, T, J], F32, name="y")
             if t % 2 == 0:
-                cb_t[b] = ps2.tile([P, 2, J], F32, name="cb")
+                cb_t[(b, t // 2)] = ps2.tile([P, 2, J], F32, name="cb")
             zqc, zqs = zq_t[b]
             taps = [k for k in range(KT) if t - (KT - 1) + k >= 0]
             for k in taps:
                 tz = t - (KT - 1) + k
                 nc.tensor.matmul_mx(
-                    out=cb_t[b][:, t % 2],
+                    out=cb_t[(b, t // 2)][:, t % 2],
                     lhsT=zqc[:, tz].bitcast(FP8X4),
                     lhsT_scale=zqs[:, tz],
                     rhs=wq[:, k].bitcast(FP8X4),
@@ -177,73 +219,98 @@ def tile_conv_st_pa_kernel(tc, inputs, supports, weights, biases, out):
                     start=(k == taps[0]),
                     stop=(k == taps[-1]),
                 )
-            if t % 2 == 1:
-                nc.vector.tensor_tensor(
-                    out=y_t[b][:, t - 1:t + 1],
-                    in0=cb_t[b][:],
-                    in1=bb[:].unsqueeze(1).to_broadcast([P, 2, J]),
-                    op=ALU.add,
-                )
+
+        def add_bias_res(b, h):
+            y_t[(b, h)] = y_pool.tile([P, 2, 2, C], F32, name="y")
+            r0 = b * NPAIR + h
+            last = NB * NPAIR
+            nc.vector.tensor_tensor(
+                out=y_t[(b, h)][:],
+                in0=cb_t[(b, h)][:].rearrange("p t (g c) -> p g t c", g=2),
+                in1=xb[:, r0:last + 1:last - r0, :].rearrange("p g (t c) -> p g t c", t=2),
+                op=ALU.add,
+            )
+
+        def gate(b, h):
+            y = y_t[(b, h)]
+            nc.scalar.activation(out=y[:, 1], in_=y[:, 1], func=ACT.Sigmoid)
 
         ov = out.rearrange("a t (b p) c -> p b (a t) c", p=P)
-        ot_t = {}
 
-        def epilogue(b, g):
-            t0, t1 = EPI[g]
-            y = y_t[b]
-            if g == 0:
-                ot_t[b] = y_pool.tile([P, T, C], F32, name="ot")
-            nc.scalar.activation(out=y[:, t0:t1, C:J], in_=y[:, t0:t1, C:J], func=ACT.Sigmoid)
-            nc.vector.tensor_tensor(
-                out=y[:, t0:t1, 0:C], in0=y[:, t0:t1, 0:C], in1=x_raw[:, t0:t1, b, :], op=ALU.add)
-            nc.vector.tensor_tensor(
-                out=ot_t[b][:, t0:t1], in0=y[:, t0:t1, 0:C], in1=y[:, t0:t1, C:J], op=ALU.mult)
-            if g == len(EPI) - 1:
-                nc.sync.dma_start(out=ov[:, b], in_=ot_t[b][:])
+        def product(b, h):
+            if h == 0:
+                ot_t[b] = ot_pool.tile([P, T, C], F32, name="ot")
+            y = y_t[(b, h)]
+            eng = nc.gpsimd if V3_GP else nc.vector
+            eng.tensor_tensor(out=ot_t[b][:, 2 * h:2 * h + 2], in0=y[:, 0], in1=y[:, 1], op=ALU.mult)
+            if b == NB - 1:
+                nc.sync.dma_start(out=ov[:, b, 2 * h:2 * h + 2], in_=ot_t[b][:, 2 * h:2 * h + 2])
+            elif h == NPAIR - 1:
+                nc.gpsimd.dma_start(out=ov[:, b], in_=ot_t[b][:])
 
-        prep_x(0, nc.vector.tensor_copy)
-        regroup_s(0, 0, nc.vector.tensor_copy)
-        regroup_s(0, 1, nc.scalar.copy)
+        VC = nc.vector.tensor_copy
+        SC = nc.scalar.copy
+
+        prep_bias()
+        regroup_x(0, SC)
+        make_xb(0)
         quant_x(0)
-        quant_s(0, 0)
-        prep_x(1, nc.scalar.copy)
-        prep_x(2, nc.vector.tensor_copy)
-        quant_s(0, 1)
+        regroup_x(1, SC)
+        make_xb(1)
         quant_x(1)
+        regroup_x(2, SC)
+        make_xb(2)
         quant_x(2)
-        bps = ps2.tile([P, 2, J], F32, name="cb")
-        nc.tensor.matmul(out=bps[:, 0], lhsT=ones[:], rhs=brow[:], start=True, stop=True)
-        nc.vector.tensor_copy(out=bb[:], in_=bps[:, 0])
-        nc.scalar.copy(
-            out=wg[:].rearrange("p k (c i) j -> p k c j i", i=4),
-            in_=w_raw[:].rearrange("p k j (c i) -> p k c j i", i=4),
-        )
-        nc.vector.quantize_mx(
-            out=wq[:, 0:2].rearrange("p k n -> p (k n)").bitcast(FP8X4),
-            scales=ws[:, 0:2].rearrange("p k n -> p (k n)"),
-            in_=wg[:, 0:2].rearrange("p k n j -> p (k n j)"),
-        )
-        nc.vector.quantize_mx(
-            out=wq[:, 2].bitcast(FP8X4),
-            scales=ws[:, 2],
-            in_=wg[:, 2].rearrange("p n j -> p (n j)"),
-        )
+        regroup_s(0, 0, 0, ORDER, VC)
+        regroup_s(1, 0, 0, ORDER, SC)
+        quant_s(0, 0)
+        quant_s(1, 0)
+        regroup_s(0, 1, 0, ORDER, VC)
+        regroup_s(1, 1, 0, ORDER, SC)
+        quant_s(0, 1)
 
-        for s in range(NB + 1):
-            for t in range(T):
-                if s + 1 < NB:
-                    if t == 0:
-                        regroup_s(s + 1, 0, nc.vector.tensor_copy)
-                    if t == 1:
-                        regroup_s(s + 1, 1, nc.scalar.copy)
-                    if t == 2:
-                        quant_s(s + 1, 0)
-                    if t == 4:
-                        quant_s(s + 1, 1)
-                if s < NB:
-                    step1(s, t)
-                if s >= 1:
-                    step2(s - 1, t)
-                    for g, (t0, t1) in enumerate(EPI):
-                        if t == t1 - 1:
-                            epilogue(s - 1, g)
+        prep = {}
+
+        def at(slot, fn, *args):
+            if slot not in prep:
+                prep[slot] = []
+            prep[slot].append((fn, args))
+
+        for b in range(2, NB):
+            base = PREP_BASE[b]
+            ns = NS[b]
+            at(base, regroup_s, b, 0, 0, ORDER, VC)
+            if ns < ORDER:
+                at(base + 1, regroup_s, b, 1, 0, ORDER - ns, VC)
+            for i in range(ns):
+                at(base + 1 + i, regroup_s, b, 1, ORDER - 1 - i, ORDER - i, SC)
+            at(base + 2, quant_s, b, 0)
+            at(base + 5, quant_s, b, 1)
+        at(0, regroup_w, 2, VC)
+        at(0, quant_s, 1, 1)
+        at(1, quant_w, 2)
+        at(1, regroup_w, 1, VC)
+        at(2, quant_w, 1)
+        at(2, regroup_w, 0, VC)
+        at(3, quant_w, 0)
+
+        for g in range(NB * T + L2 + 4):
+            for fn, args in prep.get(g, []):
+                fn(*args)
+            if g < NB * T:
+                step1(g // T, g % T)
+            i = g - 1
+            if 0 <= i < NB * T and i % 2 == 1:
+                quant_z(i // T, (i % T) // 2)
+            i = g - L2
+            if 0 <= i < NB * T:
+                step2(i // T, i % T)
+            i = g - L2 - 1
+            if 0 <= i < NB * T and i % 2 == 1:
+                add_bias_res(i // T, (i % T) // 2)
+            i = g - L2 - 2
+            if 0 <= i < NB * T and i % 2 == 1:
+                gate(i // T, (i % T) // 2)
+            i = g - L2 - 3
+            if 0 <= i < NB * T and i % 2 == 1:
+                product(i // T, (i % T) // 2)

@@ -1,6 +1,7 @@
 from contextlib import ExitStack
 
 import concourse.mybir as mybir
+from concourse.masks import make_identity
 
 BF16 = mybir.dt.bfloat16
 F32 = mybir.dt.float32
@@ -30,7 +31,6 @@ BPC = CW // P
 PREP_BASE = [0,0,6,10,16,22,29,35]
 NS = [0,0,2,3,3,3,3,3]
 V3_GP = False
-XB_GP = False
 
 
 def tile_conv_st_pa_kernel(tc, inputs, supports, weights, biases, out):
@@ -50,8 +50,13 @@ def tile_conv_st_pa_kernel(tc, inputs, supports, weights, biases, out):
 
         ones = keep.tile([P, P], BF16, name="ones")
         nc.vector.memset(ones[:], 1.0)
+        ident = keep.tile([P, P], BF16, name="ident")
+        make_identity(nc, ident[:])
         brow = keep.tile([P, J], BF16, name="brow")
         nc.vector.memset(brow[:], 0.0)
+
+        warm = keep.tile([P, 1], F32, name="warm")
+        nc.scalar.activation(out=warm[:], in_=ones[:, 0:1], func=ACT.Sigmoid)
 
         x_raw = keep.tile([P, T, NB, C], BF16, name="x_raw")
         xv = inputs.rearrange("a t (b p) c -> p (a t) b c", p=P)
@@ -77,8 +82,8 @@ def tile_conv_st_pa_kernel(tc, inputs, supports, weights, biases, out):
                 in_=weights.rearrange("(k p j) n -> p k (j n)", k=KT, p=P, j=ORDER),
             )
 
-        nc.sync.dma_start(out=brow[0:1, :], in_=biases.rearrange("(a n) -> a n", a=1))
         load_x(0)
+        nc.sync.dma_start(out=brow[0:1, :], in_=biases.rearrange("(a n) -> a n", a=1))
         load_x(1)
         load_x(2)
         load_s(0, 0)
@@ -92,7 +97,6 @@ def tile_conv_st_pa_kernel(tc, inputs, supports, weights, biases, out):
         xq = keep.tile([P, T, KP, C], U32, name="xq", align_bytes=64)
         xs = keep.tile([P, T, KP, C], U8, name="xs", align_bytes=64)
         xb = keep.tile([P, NB * NPAIR + 1, 2 * C], F32, name="xb")
-        bv = keep.tile([P, C], F32, name="bv")
         wg = keep.tile([P, KT, J, 4], BF16, name="wg", align_bytes=64)
         wq = keep.tile([P, KT, J], U32, name="wq", align_bytes=64)
         ws = keep.tile([P, KT, J], U8, name="ws", align_bytes=64)
@@ -112,19 +116,27 @@ def tile_conv_st_pa_kernel(tc, inputs, supports, weights, biases, out):
                 in_=xg[:, sl].rearrange("p t k c j -> p (t k c j)"),
             )
 
-        def make_xb(h):
-            eng = nc.gpsimd if XB_GP else nc.vector
-            eng.tensor_tensor(
-                out=xb[:, h:NB * NPAIR:NPAIR, :].rearrange("p b (t c) -> p b t c", t=2),
-                in0=x_raw[:, 2 * h:2 * h + 2].rearrange("p t b c -> p b t c"),
-                in1=bv[:].unsqueeze(1).unsqueeze(1).to_broadcast([P, NB, 2, C]),
-                op=ALU.add,
+        def make_xb(t, b0):
+            bank = ps2.tile([P, 2, J], F32, name="cb")
+            rows = bank[:].rearrange("p a (b c) -> p (a b) c", c=C)
+            nc.tensor.matmul(
+                out=rows,
+                lhsT=ones[:],
+                rhs=brow[:, 0:C].unsqueeze(1).to_broadcast([P, 4, C]),
+                start=True,
+                stop=False,
+            )
+            nc.tensor.matmul(out=rows, lhsT=ident[:], rhs=x_raw[:, t, b0:b0 + 4, :], start=False, stop=True)
+            h, tt = divmod(t, 2)
+            r0 = b0 * NPAIR + h
+            nc.scalar.copy(
+                out=xb[:, r0:r0 + 3 * NPAIR + 1:NPAIR, tt * C:(tt + 1) * C],
+                in_=rows,
             )
 
         def prep_bias():
             bps = ps2.tile([P, 2, J], F32, name="cb")
             nc.tensor.matmul(out=bps[:, 0], lhsT=ones[:], rhs=brow[:], start=True, stop=True)
-            nc.vector.tensor_copy(out=bv[:], in_=bps[:, 0, 0:C])
             nc.vector.tensor_copy(
                 out=xb[:, NB * NPAIR, :].rearrange("p (t c) -> p t c", t=2),
                 in_=bps[:, 0, C:J].unsqueeze(1).to_broadcast([P, 2, C]),
@@ -251,23 +263,24 @@ def tile_conv_st_pa_kernel(tc, inputs, supports, weights, biases, out):
         VC = nc.vector.tensor_copy
         SC = nc.scalar.copy
 
-        prep_bias()
-        regroup_x(0, SC)
-        make_xb(0)
+        regroup_x(0, VC)
+        regroup_x(1, VC)
         quant_x(0)
-        regroup_x(1, SC)
-        make_xb(1)
+        prep_bias()
+        regroup_x(2, VC)
         quant_x(1)
-        regroup_x(2, SC)
-        make_xb(2)
         quant_x(2)
+        for b0 in (0, 4):
+            for t in range(T):
+                make_xb(t, b0)
         regroup_s(0, 0, 0, ORDER, VC)
-        regroup_s(1, 0, 0, ORDER, SC)
+        regroup_s(0, 1, 2, ORDER, SC)
         quant_s(0, 0)
-        quant_s(1, 0)
-        regroup_s(0, 1, 0, ORDER, VC)
-        regroup_s(1, 1, 0, ORDER, SC)
+        regroup_s(0, 1, 0, 2, VC)
         quant_s(0, 1)
+        regroup_s(1, 0, 0, ORDER, SC)
+        quant_s(1, 0)
+        regroup_s(1, 1, 0, ORDER, VC)
 
         prep = {}
 

@@ -59,21 +59,24 @@ def tile_conv_st_pa_kernel(tc, inputs, supports, weights, biases, out):
         nc.scalar.activation(out=warm[:], in_=ones[:, 0:1], func=ACT.Sigmoid)
 
         x_raw = keep.tile([P, T, NB, C], BF16, name="x_raw")
-        xv = inputs.rearrange("a t (b p) c -> p (a t) b c", p=P)
-        sv = supports.rearrange("(b p) (o n) -> p b o n", p=P, o=ORDER)
+        xv = inputs.rearrange("a t (h p e) c -> p (a t h) (e c)", p=P, e=2)
+        sv = supports.rearrange("(h p e) (o n) -> p h e o n", p=P, e=2, o=ORDER)
         s_raw = []
         for ci in range(NCH):
             s_raw.append(keep.tile([P, NB, ORDER, CW], BF16, name="s_raw%d" % ci))
         w_raw = keep.tile([P, KT, ORDER, J], BF16, name="w_raw")
 
         def load_x(h):
-            nc.sync.dma_start(out=x_raw[:, 2 * h:2 * h + 2], in_=xv[:, 2 * h:2 * h + 2])
+            nc.sync.dma_start(
+                out=x_raw[:, 2 * h:2 * h + 2].rearrange("p t (h e) c -> p (t h) (e c)", e=2),
+                in_=xv[:, 8 * h:8 * h + 8],
+            )
 
         def load_s(ci, kp):
-            for o in range(ORDER):
+            for r in range(4 * kp, 4 * kp + 4):
                 nc.sync.dma_start(
-                    out=s_raw[ci][:, 4 * kp:4 * kp + 4, o, :],
-                    in_=sv[:, 4 * kp:4 * kp + 4, o, ci * CW:(ci + 1) * CW],
+                    out=s_raw[ci][:, r],
+                    in_=sv[:, r // 2, r % 2, :, ci * CW:(ci + 1) * CW],
                 )
 
         def load_w():
@@ -164,7 +167,7 @@ def tile_conv_st_pa_kernel(tc, inputs, supports, weights, biases, out):
             ci, q = divmod(b, BPC)
             eng_copy(
                 out=grp_t[b][:, kp, o0:o1].rearrange("p o (c i) j -> p o c j i", i=4),
-                in_=s_raw[ci][:, 4 * kp:4 * kp + 4, o0:o1, q * P:(q + 1) * P].rearrange(
+                in_=s_raw[ci][:, 4 * kp:4 * kp + 4, o0:o1, q:CW:2].rearrange(
                     "p j o (c i) -> p o c j i", i=4),
             )
 
@@ -247,7 +250,7 @@ def tile_conv_st_pa_kernel(tc, inputs, supports, weights, biases, out):
             y = y_t[(b, h)]
             nc.scalar.activation(out=y[:, 1], in_=y[:, 1], func=ACT.Sigmoid)
 
-        ov = out.rearrange("a t (b p) c -> p b (a t) c", p=P)
+        ov = out.rearrange("a t (h p e) c -> p h e (a t) c", p=P, e=2)
 
         def product(b, h):
             if h == 0:
@@ -256,9 +259,9 @@ def tile_conv_st_pa_kernel(tc, inputs, supports, weights, biases, out):
             eng = nc.gpsimd if V3_GP else nc.vector
             eng.tensor_tensor(out=ot_t[b][:, 2 * h:2 * h + 2], in0=y[:, 0], in1=y[:, 1], op=ALU.mult)
             if b == NB - 1:
-                nc.sync.dma_start(out=ov[:, b, 2 * h:2 * h + 2], in_=ot_t[b][:, 2 * h:2 * h + 2])
+                nc.sync.dma_start(out=ov[:, b // 2, b % 2, 2 * h:2 * h + 2], in_=ot_t[b][:, 2 * h:2 * h + 2])
             elif h == NPAIR - 1:
-                nc.gpsimd.dma_start(out=ov[:, b], in_=ot_t[b][:])
+                nc.sync.dma_start(out=ov[:, b // 2, b % 2], in_=ot_t[b][:])
 
         VC = nc.vector.tensor_copy
         SC = nc.scalar.copy

@@ -29,7 +29,7 @@ CW = 256
 NCH = NODES // CW
 BPC = CW // P
 PREP_BASE = [0,0,6,10,16,22,29,35]
-NS = [0,0,2,3,3,3,3,3]
+NS = [0, 0, 3, 3, 3, 3, 3, 3]
 V3_GP = False
 
 
@@ -66,10 +66,10 @@ def tile_conv_st_pa_kernel(tc, inputs, supports, weights, biases, out):
             s_raw.append(keep.tile([P, NB, ORDER, CW], BF16, name="s_raw%d" % ci))
         w_raw = keep.tile([P, KT, ORDER, J], BF16, name="w_raw")
 
-        def load_x(h):
+        def load_x(t0, t1):
             nc.sync.dma_start(
-                out=x_raw[:, 2 * h:2 * h + 2].rearrange("p t (h e) c -> p (t h) (e c)", e=2),
-                in_=xv[:, 8 * h:8 * h + 8],
+                out=x_raw[:, t0:t1].rearrange("p t (h e) c -> p (t h) (e c)", e=2),
+                in_=xv[:, 4 * t0:4 * t1],
             )
 
         def load_s(ci, kp):
@@ -85,12 +85,13 @@ def tile_conv_st_pa_kernel(tc, inputs, supports, weights, biases, out):
                 in_=weights.rearrange("(k p j) n -> p k (j n)", k=KT, p=P, j=ORDER),
             )
 
-        load_x(0)
+        load_x(0, 1)
         nc.sync.dma_start(out=brow[0:1, :], in_=biases.rearrange("(a n) -> a n", a=1))
-        load_x(1)
-        load_x(2)
+        load_x(1, 2)
+        load_x(2, 4)
         load_s(0, 0)
         load_s(0, 1)
+        load_x(4, 6)
         load_w()
         for ci in range(1, NCH):
             load_s(ci, 0)
@@ -104,8 +105,8 @@ def tile_conv_st_pa_kernel(tc, inputs, supports, weights, biases, out):
         wq = keep.tile([P, KT, J], U32, name="wq", align_bytes=64)
         ws = keep.tile([P, KT, J], U8, name="ws", align_bytes=64)
 
-        def regroup_x(h, eng_copy):
-            sl = slice(2 * h, 2 * h + 2)
+        def regroup_x(t0, t1, eng_copy):
+            sl = slice(t0, t1)
             eng_copy(
                 out=xg[:, sl].rearrange("p t k (c i) j -> p (t k) c j i", i=4),
                 in_=x_raw[:, sl].rearrange("p t (k j) (c i) -> p (t k) c j i", j=4, i=4),
@@ -209,81 +210,99 @@ def tile_conv_st_pa_kernel(tc, inputs, supports, weights, biases, out):
                 )
             nc.scalar.copy(out=z_t[b][:, t], in_=bank[:].rearrange("p (o n) -> p n o", o=ORDER))
 
-        def quant_z(b, h):
-            sl = slice(2 * h, 2 * h + 2)
+        def first_of(b, t):
+            if b == NB - 1 and t >= T - 2:
+                return t
+            return t - 1 if t % 2 == 1 else None
+
+        def quant_z(b, t0, t):
             zqc, zqs = zq_t[b]
             nc.vector.quantize_mx(
-                out=zqc[:, sl].rearrange("p t n -> p (t n)").bitcast(FP8X4),
-                scales=zqs[:, sl].rearrange("p t n -> p (t n)"),
-                in_=z_t[b][:, sl].rearrange("p t n o -> p (t n o)"),
+                out=zqc[:, t0:t + 1].rearrange("p t n -> p (t n)").bitcast(FP8X4),
+                scales=zqs[:, t0:t + 1].rearrange("p t n -> p (t n)"),
+                in_=z_t[b][:, t0:t + 1].rearrange("p t n o -> p (t n o)"),
             )
 
-        def step2(b, t):
-            if t % 2 == 0:
-                cb_t[(b, t // 2)] = ps2.tile([P, 2, J], F32, name="cb")
+        def step2(b, t0, t):
+            bank = ps2.tile([P, 2, J], F32, name="cb")
+            cb_t[(b, t0)] = bank
             zqc, zqs = zq_t[b]
-            taps = [k for k in range(KT) if t - (KT - 1) + k >= 0]
-            for k in taps:
-                tz = t - (KT - 1) + k
-                nc.tensor.matmul_mx(
-                    out=cb_t[(b, t // 2)][:, t % 2],
-                    lhsT=zqc[:, tz].bitcast(FP8X4),
-                    lhsT_scale=zqs[:, tz],
-                    rhs=wq[:, k].bitcast(FP8X4),
-                    rhs_scale=ws[:, k],
-                    start=(k == taps[0]),
-                    stop=(k == taps[-1]),
-                )
+            for i, tt in enumerate(range(t0, t + 1)):
+                taps = [k for k in range(KT) if tt - (KT - 1) + k >= 0]
+                for k in taps:
+                    tz = tt - (KT - 1) + k
+                    nc.tensor.matmul_mx(
+                        out=bank[:, i],
+                        lhsT=zqc[:, tz].bitcast(FP8X4),
+                        lhsT_scale=zqs[:, tz],
+                        rhs=wq[:, k].bitcast(FP8X4),
+                        rhs_scale=ws[:, k],
+                        start=(k == taps[0]),
+                        stop=(k == taps[-1]),
+                    )
 
-        def add_bias_res(b, h):
-            y_t[(b, h)] = y_pool.tile([P, 2, 2, C], F32, name="y")
-            r0 = b * NPAIR + h
+        def add_bias_res(b, t0, t):
+            y = y_pool.tile([P, 2, 2, C], F32, name="y")
+            y_t[(b, t0)] = y
+            r0 = b * NPAIR + t0 // 2
             last = NB * NPAIR
+            n = t + 1 - t0
             nc.vector.tensor_tensor(
-                out=y_t[(b, h)][:],
-                in0=cb_t[(b, h)][:].rearrange("p t (g c) -> p g t c", g=2),
-                in1=xb[:, r0:last + 1:last - r0, :].rearrange("p g (t c) -> p g t c", t=2),
+                out=y[:, :, 0:n],
+                in0=cb_t[(b, t0)][:, 0:n].rearrange("p t (g c) -> p g t c", g=2),
+                in1=xb[:, r0:last + 1:last - r0, :].rearrange("p g (t c) -> p g t c", t=2)[:, :, t0 % 2:t0 % 2 + n],
                 op=ALU.add,
             )
 
-        def gate(b, h):
-            y = y_t[(b, h)]
-            nc.scalar.activation(out=y[:, 1], in_=y[:, 1], func=ACT.Sigmoid)
+        def gate(b, t0, t):
+            n = t + 1 - t0
+            y = y_t[(b, t0)]
+            nc.scalar.activation(out=y[:, 1, 0:n], in_=y[:, 1, 0:n], func=ACT.Sigmoid)
 
         ov = out.rearrange("a t (h p e) c -> p h e (a t) c", p=P, e=2)
 
-        def product(b, h):
-            if h == 0:
+        def product(b, t0, t):
+            if t0 == 0:
                 ot_t[b] = ot_pool.tile([P, T, C], F32, name="ot")
-            y = y_t[(b, h)]
-            eng = nc.gpsimd if V3_GP else nc.vector
-            eng.tensor_tensor(out=ot_t[b][:, 2 * h:2 * h + 2], in0=y[:, 0], in1=y[:, 1], op=ALU.mult)
+            n = t + 1 - t0
+            y = y_t[(b, t0)]
+            nc.vector.tensor_tensor(out=ot_t[b][:, t0:t + 1], in0=y[:, 0, 0:n], in1=y[:, 1, 0:n], op=ALU.mult)
             if b == NB - 1:
-                nc.sync.dma_start(out=ov[:, b // 2, b % 2, 2 * h:2 * h + 2], in_=ot_t[b][:, 2 * h:2 * h + 2])
-            elif h == NPAIR - 1:
+                nc.sync.dma_start(out=ov[:, b // 2, b % 2, t0:t + 1], in_=ot_t[b][:, t0:t + 1])
+            elif t == T - 1:
                 nc.sync.dma_start(out=ov[:, b // 2, b % 2], in_=ot_t[b][:])
 
         VC = nc.vector.tensor_copy
         SC = nc.scalar.copy
 
-        regroup_x(0, VC)
-        regroup_x(1, VC)
-        quant_x(0)
-        prep_bias()
-        regroup_x(2, VC)
-        quant_x(1)
-        quant_x(2)
-        for b0 in (0, 4):
-            for t in range(T):
-                make_xb(t, b0)
-        regroup_s(0, 0, 0, ORDER, VC)
-        regroup_s(0, 1, 2, ORDER, SC)
-        quant_s(0, 0)
-        regroup_s(0, 1, 0, 2, VC)
-        quant_s(0, 1)
-        regroup_s(1, 0, 0, ORDER, SC)
-        quant_s(1, 0)
-        regroup_s(1, 1, 0, ORDER, VC)
+        with tc.manual_schedule(engines={mybir.EngineType.Activation}):
+            prep_bias()
+            regroup_x(0, 1, VC)
+            regroup_x(1, 2, VC)
+            for t in (0, 1):
+                make_xb(t, 0)
+                make_xb(t, 4)
+            regroup_x(2, 4, VC)
+            quant_x(0)
+            for t in (2, 3):
+                make_xb(t, 0)
+                make_xb(t, 4)
+            quant_x(1)
+            regroup_s(0, 0, 0, ORDER, VC)
+            quant_s(0, 0)
+            regroup_s(1, 0, 2, ORDER, SC)
+            regroup_s(1, 0, 0, 2, VC)
+            regroup_s(0, 1, 0, 2, VC)
+            regroup_s(0, 1, 2, ORDER, SC)
+            quant_s(0, 1)
+            quant_s(1, 0)
+            regroup_s(1, 1, 0, 2, VC)
+            regroup_s(1, 1, 2, ORDER, SC)
+            regroup_x(4, 6, VC)
+            quant_x(2)
+            for t in (4, 5):
+                make_xb(t, 0)
+                make_xb(t, 4)
 
         prep = {}
 
@@ -315,18 +334,7 @@ def tile_conv_st_pa_kernel(tc, inputs, supports, weights, biases, out):
                 fn(*args)
             if g < NB * T:
                 step1(g // T, g % T)
-            i = g - 1
-            if 0 <= i < NB * T and i % 2 == 1:
-                quant_z(i // T, (i % T) // 2)
-            i = g - L2
-            if 0 <= i < NB * T:
-                step2(i // T, i % T)
-            i = g - L2 - 1
-            if 0 <= i < NB * T and i % 2 == 1:
-                add_bias_res(i // T, (i % T) // 2)
-            i = g - L2 - 2
-            if 0 <= i < NB * T and i % 2 == 1:
-                gate(i // T, (i % T) // 2)
-            i = g - L2 - 3
-            if 0 <= i < NB * T and i % 2 == 1:
-                product(i // T, (i % T) // 2)
+            for lag, stage in ((1, quant_z), (L2, step2), (L2 + 1, add_bias_res), (L2 + 2, gate), (L2 + 3, product)):
+                b, t = divmod(g - lag, T)
+                if 0 <= b < NB and first_of(b, t) is not None:
+                    stage(b, first_of(b, t), t)

@@ -59,8 +59,8 @@ def tile_conv_st_pa_kernel(tc, inputs, supports, weights, biases, out):
         nc.scalar.activation(out=warm[:], in_=ones[:, 0:1], func=ACT.Sigmoid)
 
         x_raw = keep.tile([P, T, NB, C], BF16, name="x_raw")
-        xv = inputs.rearrange("a t (h p e) c -> p (a t h) (e c)", p=P, e=2)
-        sv = supports.rearrange("(h p e) (o n) -> p h e o n", p=P, e=2, o=ORDER)
+        xv = inputs.rearrange("a t (b p) c -> p (a t b) c", p=P)
+        sv = supports.rearrange("(b p) (o n) -> p b o n", p=P, o=ORDER)
         s_raw = []
         for ci in range(NCH):
             s_raw.append(keep.tile([P, NB, ORDER, CW], BF16, name="s_raw%d" % ci))
@@ -68,15 +68,15 @@ def tile_conv_st_pa_kernel(tc, inputs, supports, weights, biases, out):
 
         def load_x(t0, t1):
             nc.sync.dma_start(
-                out=x_raw[:, t0:t1].rearrange("p t (h e) c -> p (t h) (e c)", e=2),
-                in_=xv[:, 4 * t0:4 * t1],
+                out=x_raw[:, t0:t1].rearrange("p t b c -> p (t b) c"),
+                in_=xv[:, NB * t0:NB * t1],
             )
 
         def load_s(ci, kp):
             for r in range(4 * kp, 4 * kp + 4):
                 nc.sync.dma_start(
                     out=s_raw[ci][:, r],
-                    in_=sv[:, r // 2, r % 2, :, ci * CW:(ci + 1) * CW],
+                    in_=sv[:, r, :, ci * CW:(ci + 1) * CW],
                 )
 
         def load_w():
@@ -108,8 +108,8 @@ def tile_conv_st_pa_kernel(tc, inputs, supports, weights, biases, out):
         def regroup_x(t0, t1, eng_copy):
             sl = slice(t0, t1)
             eng_copy(
-                out=xg[:, sl].rearrange("p t k (c i) j -> p (t k) c j i", i=4),
-                in_=x_raw[:, sl].rearrange("p t (k j) (c i) -> p (t k) c j i", j=4, i=4),
+                out=xg[:, sl].rearrange("p t k c j -> p (t k) c j"),
+                in_=x_raw[:, sl].rearrange("p t (k j) c -> p (t k) c j", j=4),
             )
 
         def quant_x(h):
@@ -148,8 +148,8 @@ def tile_conv_st_pa_kernel(tc, inputs, supports, weights, biases, out):
 
         def regroup_w(k, eng_copy):
             eng_copy(
-                out=wg[:, k].rearrange("p (c i) j -> p c j i", i=4),
-                in_=w_raw[:, k].rearrange("p j (c i) -> p c j i", i=4),
+                out=wg[:, k],
+                in_=w_raw[:, k].rearrange("p j n -> p n j"),
             )
 
         def quant_w(k):
@@ -167,9 +167,8 @@ def tile_conv_st_pa_kernel(tc, inputs, supports, weights, biases, out):
                 grp_t[b] = grp_pool.tile([P, KP, ORDER, P, 4], BF16, name="grp", align_bytes=64)
             ci, q = divmod(b, BPC)
             eng_copy(
-                out=grp_t[b][:, kp, o0:o1].rearrange("p o (c i) j -> p o c j i", i=4),
-                in_=s_raw[ci][:, 4 * kp:4 * kp + 4, o0:o1, q:CW:2].rearrange(
-                    "p j o (c i) -> p o c j i", i=4),
+                out=grp_t[b][:, kp, o0:o1],
+                in_=s_raw[ci][:, 4 * kp:4 * kp + 4, o0:o1, q * P:(q + 1) * P].rearrange("p j o n -> p o n j"),
             )
 
         def quant_s(b, kp):
@@ -259,7 +258,7 @@ def tile_conv_st_pa_kernel(tc, inputs, supports, weights, biases, out):
             y = y_t[(b, t0)]
             nc.scalar.activation(out=y[:, 1, 0:n], in_=y[:, 1, 0:n], func=ACT.Sigmoid)
 
-        ov = out.rearrange("a t (h p e) c -> p h e (a t) c", p=P, e=2)
+        ov = out.rearrange("a t (b p) c -> p b (a t) c", p=P)
 
         def product(b, t0, t):
             if t0 == 0:
@@ -268,9 +267,9 @@ def tile_conv_st_pa_kernel(tc, inputs, supports, weights, biases, out):
             y = y_t[(b, t0)]
             nc.vector.tensor_tensor(out=ot_t[b][:, t0:t + 1], in0=y[:, 0, 0:n], in1=y[:, 1, 0:n], op=ALU.mult)
             if b == NB - 1:
-                nc.sync.dma_start(out=ov[:, b // 2, b % 2, t0:t + 1], in_=ot_t[b][:, t0:t + 1])
+                nc.sync.dma_start(out=ov[:, b, t0:t + 1], in_=ot_t[b][:, t0:t + 1])
             elif t == T - 1:
-                nc.sync.dma_start(out=ov[:, b // 2, b % 2], in_=ot_t[b][:])
+                nc.sync.dma_start(out=ov[:, b], in_=ot_t[b][:])
 
         VC = nc.vector.tensor_copy
         SC = nc.scalar.copy

@@ -29,7 +29,7 @@ CW = 256
 NCH = NODES // CW
 BPC = CW // P
 PREP_BASE = [0,0,6,10,16,22,29,35]
-NS = [0, 0, 3, 3, 3, 3, 3, 3]
+NS = [0, 0, 3, 4, 3, 4, 3, 4]
 V3_GP = False
 
 
@@ -108,8 +108,8 @@ def tile_conv_st_pa_kernel(tc, inputs, supports, weights, biases, out):
         def regroup_x(t0, t1, eng_copy):
             sl = slice(t0, t1)
             eng_copy(
-                out=xg[:, sl].rearrange("p t k c j -> p (t k) c j"),
-                in_=x_raw[:, sl].rearrange("p t (k j) c -> p (t k) c j", j=4),
+                out=xg[:, sl].rearrange("p t k (c i) j -> p (t k) c j i", i=4),
+                in_=x_raw[:, sl].rearrange("p t (k j) (c i) -> p (t k) c j i", j=4, i=4),
             )
 
         def quant_x(h):
@@ -148,8 +148,8 @@ def tile_conv_st_pa_kernel(tc, inputs, supports, weights, biases, out):
 
         def regroup_w(k, eng_copy):
             eng_copy(
-                out=wg[:, k],
-                in_=w_raw[:, k].rearrange("p j n -> p n j"),
+                out=wg[:, k].rearrange("p (c i) j -> p c j i", i=4),
+                in_=w_raw[:, k].rearrange("p j (c i) -> p c j i", i=4),
             )
 
         def quant_w(k):
@@ -167,8 +167,9 @@ def tile_conv_st_pa_kernel(tc, inputs, supports, weights, biases, out):
                 grp_t[b] = grp_pool.tile([P, KP, ORDER, P, 4], BF16, name="grp", align_bytes=64)
             ci, q = divmod(b, BPC)
             eng_copy(
-                out=grp_t[b][:, kp, o0:o1],
-                in_=s_raw[ci][:, 4 * kp:4 * kp + 4, o0:o1, q * P:(q + 1) * P].rearrange("p j o n -> p o n j"),
+                out=grp_t[b][:, kp, o0:o1].rearrange("p o (c i) j -> p o c j i", i=4),
+                in_=s_raw[ci][:, 4 * kp:4 * kp + 4, o0:o1, q * P:(q + 1) * P].rearrange(
+                    "p j o (c i) -> p o c j i", i=4),
             )
 
         def quant_s(b, kp):

from contextlib import ExitStack

import concourse.mybir as mybir
from concourse.masks import make_identity

BF16 = mybir.dt.bfloat16
F32 = mybir.dt.float32
U32 = mybir.dt.uint32
U8 = mybir.dt.uint8
FP8X4 = mybir.dt.float8_e4m3fn_x4
ACT = mybir.ActivationFunctionType
ALU = mybir.AluOpType

P = 128
T = 6
NODES = 1024
C = 128
ORDER = 4
KT = 3
J = 2 * C
NB = NODES // P
KP = 2
NPAIR = T // 2
FLOPS = 2 * T * C * NODES * ORDER * NODES + 2 * T * NODES * KT * C * ORDER * J

MANUAL = False
L2 = 4
CW = 256
NCH = NODES // CW
BPC = CW // P
PREP_BASE = [0,0,6,10,16,22,29,35]
NS = [0, 0, 3, 4, 3, 4, 3, 4]
V3_GP = False


def tile_conv_st_pa_kernel(tc, inputs, supports, weights, biases, out):
    nc = tc.nc
    with ExitStack() as ctx:
        if MANUAL:
            ctx.enter_context(tc.manual_schedule())
        keep = ctx.enter_context(tc.tile_pool(name="keep", bufs=1))
        grp_pool = ctx.enter_context(tc.tile_pool(name="grp", bufs=3))
        sq_pool = ctx.enter_context(tc.tile_pool(name="sq", bufs=3))
        z_pool = ctx.enter_context(tc.tile_pool(name="z", bufs=2))
        zq_pool = ctx.enter_context(tc.tile_pool(name="zq", bufs=3))
        y_pool = ctx.enter_context(tc.tile_pool(name="y", bufs=4))
        ot_pool = ctx.enter_context(tc.tile_pool(name="ot", bufs=3))
        ps1 = ctx.enter_context(tc.psum_pool(name="ps1", bufs=5))
        ps2 = ctx.enter_context(tc.psum_pool(name="ps2", bufs=3))

        ones = keep.tile([P, P], BF16, name="ones")
        nc.vector.memset(ones[:], 1.0)
        ident = keep.tile([P, P], BF16, name="ident")
        make_identity(nc, ident[:])
        brow = keep.tile([P, J], BF16, name="brow")
        nc.vector.memset(brow[:], 0.0)

        warm = keep.tile([P, 1], F32, name="warm")
        nc.scalar.activation(out=warm[:], in_=ones[:, 0:1], func=ACT.Sigmoid)

        x_raw = keep.tile([P, T, NB, C], BF16, name="x_raw")
        xv = inputs.rearrange("a t (b p) c -> p (a t b) c", p=P)
        sv = supports.rearrange("(b p) (o n) -> p b o n", p=P, o=ORDER)
        s_raw = []
        for ci in range(NCH):
            s_raw.append(keep.tile([P, NB, ORDER, CW], BF16, name="s_raw%d" % ci))
        w_raw = keep.tile([P, KT, ORDER, J], BF16, name="w_raw")

        def load_x(t0, t1):
            nc.sync.dma_start(
                out=x_raw[:, t0:t1].rearrange("p t b c -> p (t b) c"),
                in_=xv[:, NB * t0:NB * t1],
            )

        def load_s(ci, kp):
            for r in range(4 * kp, 4 * kp + 4):
                nc.sync.dma_start(
                    out=s_raw[ci][:, r],
                    in_=sv[:, r, :, ci * CW:(ci + 1) * CW],
                )

        def load_w():
            nc.sync.dma_start(
                out=w_raw[:].rearrange("p k j n -> p k (j n)"),
                in_=weights.rearrange("(k p j) n -> p k (j n)", k=KT, p=P, j=ORDER),
            )

        load_x(0, 1)
        nc.sync.dma_start(out=brow[0:1, :], in_=biases.rearrange("(a n) -> a n", a=1))
        load_x(1, 2)
        load_x(2, 4)
        load_s(0, 0)
        load_s(0, 1)
        load_x(4, 6)
        load_w()
        for ci in range(1, NCH):
            load_s(ci, 0)
            load_s(ci, 1)

        xg = keep.tile([P, T, KP, C, 4], BF16, name="xg", align_bytes=64)
        xq = keep.tile([P, T, KP, C], U32, name="xq", align_bytes=64)
        xs = keep.tile([P, T, KP, C], U8, name="xs", align_bytes=64)
        xb = keep.tile([P, NB * NPAIR + 1, 2 * C], F32, name="xb")
        wg = keep.tile([P, KT, J, 4], BF16, name="wg", align_bytes=64)
        wq = keep.tile([P, KT, J], U32, name="wq", align_bytes=64)
        ws = keep.tile([P, KT, J], U8, name="ws", align_bytes=64)

        def regroup_x(t0, t1, eng_copy):
            sl = slice(t0, t1)
            eng_copy(
                out=xg[:, sl].rearrange("p t k (c i) j -> p (t k) c j i", i=4),
                in_=x_raw[:, sl].rearrange("p t (k j) (c i) -> p (t k) c j i", j=4, i=4),
            )

        def quant_x(h):
            sl = slice(2 * h, 2 * h + 2)
            nc.vector.quantize_mx(
                out=xq[:, sl].rearrange("p t k c -> p (t k c)").bitcast(FP8X4),
                scales=xs[:, sl].rearrange("p t k c -> p (t k c)"),
                in_=xg[:, sl].rearrange("p t k c j -> p (t k c j)"),
            )

        def make_xb(t, b0):
            bank = ps2.tile([P, 2, J], F32, name="cb")
            rows = bank[:].rearrange("p a (b c) -> p (a b) c", c=C)
            nc.tensor.matmul(
                out=rows,
                lhsT=ones[:],
                rhs=brow[:, 0:C].unsqueeze(1).to_broadcast([P, 4, C]),
                start=True,
                stop=False,
            )
            nc.tensor.matmul(out=rows, lhsT=ident[:], rhs=x_raw[:, t, b0:b0 + 4, :], start=False, stop=True)
            h, tt = divmod(t, 2)
            r0 = b0 * NPAIR + h
            nc.scalar.copy(
                out=xb[:, r0:r0 + 3 * NPAIR + 1:NPAIR, tt * C:(tt + 1) * C],
                in_=rows,
            )

        def prep_bias():
            bps = ps2.tile([P, 2, J], F32, name="cb")
            nc.tensor.matmul(out=bps[:, 0], lhsT=ones[:], rhs=brow[:], start=True, stop=True)
            nc.vector.tensor_copy(
                out=xb[:, NB * NPAIR, :].rearrange("p (t c) -> p t c", t=2),
                in_=bps[:, 0, C:J].unsqueeze(1).to_broadcast([P, 2, C]),
            )

        def regroup_w(k, eng_copy):
            eng_copy(
                out=wg[:, k].rearrange("p (c i) j -> p c j i", i=4),
                in_=w_raw[:, k].rearrange("p j (c i) -> p c j i", i=4),
            )

        def quant_w(k):
            nc.vector.quantize_mx(
                out=wq[:, k].bitcast(FP8X4),
                scales=ws[:, k],
                in_=wg[:, k].rearrange("p n j -> p (n j)"),
            )

        grp_t = {}
        sq_t = {}

        def regroup_s(b, kp, o0, o1, eng_copy):
            if b not in grp_t:
                grp_t[b] = grp_pool.tile([P, KP, ORDER, P, 4], BF16, name="grp", align_bytes=64)
            ci, q = divmod(b, BPC)
            eng_copy(
                out=grp_t[b][:, kp, o0:o1].rearrange("p o (c i) j -> p o c j i", i=4),
                in_=s_raw[ci][:, 4 * kp:4 * kp + 4, o0:o1, q * P:(q + 1) * P].rearrange(
                    "p j o (c i) -> p o c j i", i=4),
            )

        def quant_s(b, kp):
            if b not in sq_t:
                sqc = sq_pool.tile([P, KP, ORDER * P], U32, name="sqc", align_bytes=64)
                sqs = sq_pool.tile([P, KP, ORDER * P], U8, name="sqs", align_bytes=64)
                sq_t[b] = (sqc, sqs)
            sqc, sqs = sq_t[b]
            nc.vector.quantize_mx(
                out=sqc[:, kp].bitcast(FP8X4),
                scales=sqs[:, kp],
                in_=grp_t[b][:, kp].rearrange("p o n j -> p (o n j)"),
            )

        z_t = {}
        zq_t = {}
        y_t = {}
        cb_t = {}
        ot_t = {}

        def step1(b, t):
            if t == 0:
                z_t[b] = z_pool.tile([P, T, P, ORDER], BF16, name="zb", align_bytes=64)
                zqc = zq_pool.tile([P, T, P], U32, name="zqc", align_bytes=64)
                zqs = zq_pool.tile([P, T, P], U8, name="zqs", align_bytes=64)
                zq_t[b] = (zqc, zqs)
            sqc, sqs = sq_t[b]
            bank = ps1.tile([P, ORDER * P], F32, name="zbank")
            for kp in range(KP):
                nc.tensor.matmul_mx(
                    out=bank[:],
                    lhsT=xq[:, t, kp].bitcast(FP8X4),
                    lhsT_scale=xs[:, t, kp],
                    rhs=sqc[:, kp].bitcast(FP8X4),
                    rhs_scale=sqs[:, kp],
                    start=(kp == 0),
                    stop=(kp == KP - 1),
                )
            nc.scalar.copy(out=z_t[b][:, t], in_=bank[:].rearrange("p (o n) -> p n o", o=ORDER))

        def first_of(b, t):
            if b == NB - 1 and t >= T - 2:
                return t
            return t - 1 if t % 2 == 1 else None

        def quant_z(b, t0, t):
            zqc, zqs = zq_t[b]
            nc.vector.quantize_mx(
                out=zqc[:, t0:t + 1].rearrange("p t n -> p (t n)").bitcast(FP8X4),
                scales=zqs[:, t0:t + 1].rearrange("p t n -> p (t n)"),
                in_=z_t[b][:, t0:t + 1].rearrange("p t n o -> p (t n o)"),
            )

        def step2(b, t0, t):
            bank = ps2.tile([P, 2, J], F32, name="cb")
            cb_t[(b, t0)] = bank
            zqc, zqs = zq_t[b]
            for i, tt in enumerate(range(t0, t + 1)):
                taps = [k for k in range(KT) if tt - (KT - 1) + k >= 0]
                for k in taps:
                    tz = tt - (KT - 1) + k
                    nc.tensor.matmul_mx(
                        out=bank[:, i],
                        lhsT=zqc[:, tz].bitcast(FP8X4),
                        lhsT_scale=zqs[:, tz],
                        rhs=wq[:, k].bitcast(FP8X4),
                        rhs_scale=ws[:, k],
                        start=(k == taps[0]),
                        stop=(k == taps[-1]),
                    )

        def add_bias_res(b, t0, t):
            y = y_pool.tile([P, 2, 2, C], F32, name="y")
            y_t[(b, t0)] = y
            r0 = b * NPAIR + t0 // 2
            last = NB * NPAIR
            n = t + 1 - t0
            nc.vector.tensor_tensor(
                out=y[:, :, 0:n],
                in0=cb_t[(b, t0)][:, 0:n].rearrange("p t (g c) -> p g t c", g=2),
                in1=xb[:, r0:last + 1:last - r0, :].rearrange("p g (t c) -> p g t c", t=2)[:, :, t0 % 2:t0 % 2 + n],
                op=ALU.add,
            )

        def gate(b, t0, t):
            n = t + 1 - t0
            y = y_t[(b, t0)]
            nc.scalar.activation(out=y[:, 1, 0:n], in_=y[:, 1, 0:n], func=ACT.Sigmoid)

        ov = out.rearrange("a t (b p) c -> p b (a t) c", p=P)

        def product(b, t0, t):
            if t0 == 0:
                ot_t[b] = ot_pool.tile([P, T, C], F32, name="ot")
            n = t + 1 - t0
            y = y_t[(b, t0)]
            nc.vector.tensor_tensor(out=ot_t[b][:, t0:t + 1], in0=y[:, 0, 0:n], in1=y[:, 1, 0:n], op=ALU.mult)
            if b == NB - 1:
                nc.sync.dma_start(out=ov[:, b, t0:t + 1], in_=ot_t[b][:, t0:t + 1])
            elif t == T - 1:
                nc.sync.dma_start(out=ov[:, b], in_=ot_t[b][:])

        VC = nc.vector.tensor_copy
        SC = nc.scalar.copy

        with tc.manual_schedule(engines={mybir.EngineType.Activation}):
            prep_bias()
            regroup_x(0, 1, VC)
            regroup_x(1, 2, VC)
            for t in (0, 1):
                make_xb(t, 0)
                make_xb(t, 4)
            regroup_x(2, 4, VC)
            quant_x(0)
            for t in (2, 3):
                make_xb(t, 0)
                make_xb(t, 4)
            quant_x(1)
            regroup_s(0, 0, 0, ORDER, VC)
            quant_s(0, 0)
            regroup_s(1, 0, 2, ORDER, SC)
            regroup_s(1, 0, 0, 2, VC)
            regroup_s(0, 1, 0, 2, VC)
            regroup_s(0, 1, 2, ORDER, SC)
            quant_s(0, 1)
            quant_s(1, 0)
            regroup_s(1, 1, 0, 2, VC)
            regroup_s(1, 1, 2, ORDER, SC)
            regroup_x(4, 6, VC)
            quant_x(2)
            for t in (4, 5):
                make_xb(t, 0)
                make_xb(t, 4)

        prep = {}

        def at(slot, fn, *args):
            if slot not in prep:
                prep[slot] = []
            prep[slot].append((fn, args))

        for b in range(2, NB):
            base = PREP_BASE[b]
            ns = NS[b]
            at(base, regroup_s, b, 0, 0, ORDER, VC)
            if ns < ORDER:
                at(base + 1, regroup_s, b, 1, 0, ORDER - ns, VC)
            for i in range(ns):
                at(base + 1 + i, regroup_s, b, 1, ORDER - 1 - i, ORDER - i, SC)
            at(base + 2, quant_s, b, 0)
            at(base + 5, quant_s, b, 1)
        at(0, regroup_w, 2, VC)
        at(0, quant_s, 1, 1)
        at(1, quant_w, 2)
        at(1, regroup_w, 1, VC)
        at(2, quant_w, 1)
        at(2, regroup_w, 0, VC)
        at(3, quant_w, 0)

        for g in range(NB * T + L2 + 4):
            for fn, args in prep.get(g, []):
                fn(*args)
            if g < NB * T:
                step1(g // T, g % T)
            for lag, stage in ((1, quant_z), (L2, step2), (L2 + 1, add_bias_res), (L2 + 2, gate), (L2 + 3, product)):
                b, t = divmod(g - lag, T)
                if 0 <= b < NB and first_of(b, t) is not None:
                    stage(b, first_of(b, t), t)
